import numpy as np
import ml_dtypes


def mxq(x, axis, fmt="e4m3"):
    dtype, down = {"e4m3": (ml_dtypes.float8_e4m3fn, 7), "e5m2": (ml_dtypes.float8_e5m2, 14)}[fmt]
    v = np.moveaxis(np.asarray(x, np.float32).astype(ml_dtypes.bfloat16).astype(np.float64), axis, -1)
    blocks = v.reshape(v.shape[:-1] + (-1, 32))
    amax = np.abs(blocks).max(-1, keepdims=True)
    byte = np.maximum(np.where(amax > 0, np.frexp(amax)[1] - 1 + 127, 0) - down, 1)
    scale = np.exp2(byte - 127.0)
    codes = (blocks / scale).astype(np.float32).astype(dtype).astype(np.float64)
    return np.moveaxis((codes * scale).reshape(v.shape), -1, axis)


WIDE = False


def mx_kscale(k):
    if not WIDE:
        return np.ones(k)
    levels = np.array([10, -10, 5, -5, 0])
    if k % 512:
        return np.exp2(np.random.permutation(np.resize(levels, k // 32))).repeat(32)
    a = np.empty((k // 512, 16))
    for p in range(k // 512):
        a[p, :8] = np.random.permutation(np.resize(levels, 8))
        for g in range(8):
            far = levels[np.abs(levels - a[p, g]) >= 10]
            a[p, g + 8] = far[np.random.randint(len(far))]
    return np.exp2(a.ravel()).repeat(32)


BF16 = ml_dtypes.bfloat16


def bf(x):
    return np.asarray(x, np.float32).astype(BF16)


def f64(x):
    return np.asarray(x).astype(np.float64)


B, D, H = 8192, 2048, 32
DH = D // H
LN_EPS = 1e-5


def layernorm(x, g, b):
    mu = x.mean(-1, keepdims=True)
    var = ((x - mu) ** 2).mean(-1, keepdims=True)
    return (x - mu) / np.sqrt(var + LN_EPS) * g + b


def setup_inputs():
    s, t = mx_kscale(D), mx_kscale(D)
    return {"kv_in": bf(np.random.standard_normal((B, D)) * s),
            "q_in": bf(np.random.standard_normal((B, D))),
            "attn_w": bf(np.random.uniform(0.25, 1.0, (B, H, 1))),
            "w_v": bf(np.random.standard_normal((D, D)) / np.sqrt(D) / s[None, :] * t[:, None]),
            "b_v": bf(np.random.standard_normal(D) * 0.3 * t),
            "out_w": bf(np.random.standard_normal((D, D)) / np.sqrt(D) / t[None, :]),
            "out_b": bf(np.random.standard_normal(D) * 0.3),
            "ln_g": bf(1.0 + 0.1 * np.random.standard_normal(D)),
            "ln_b": bf(0.1 * np.random.standard_normal(D))}


def reference(kv_in, q_in, attn_w, w_v, b_v, out_w, out_b, ln_g, ln_b):
    v = ((mxq(f64(kv_in), 1, "e4m3") @ mxq(f64(w_v), 1, "e4m3").T) + f64(b_v)).reshape(B, H, DH)
    attn = (f64(attn_w) * v).reshape(B, D)
    y = (mxq(attn, 1, "e4m3") @ mxq(f64(out_w), 1, "e4m3").T) + f64(out_b)
    return layernorm(y + f64(q_in), f64(ln_g), f64(ln_b))

@@ -1,0 +1,372 @@
+from contextlib import ExitStack
+
+import concourse.mybir as mybir
+from concourse.masks import make_identity
+
+FLOPS = 2 * 2 * 8192 * 2048 * 2048
+
+F32 = mybir.dt.float32
+BF16 = mybir.dt.bfloat16
+U32 = mybir.dt.uint32
+U8 = mybir.dt.uint8
+FP8X4 = mybir.dt.float8_e4m3fn_x4
+ALU = mybir.AluOpType
+ACT = mybir.ActivationFunctionType
+
+P = 128
+D = 2048
+NSUB = 64
+LN_EPS = 1e-5
+
+SORT = True
+T7_ON_G = True
+MANUAL = True
+LAG2 = 20
+
+
+def tile_crossmodalattention_pa_l_kernel(
+    tc, kv_in, q_in, attn_w, w_v, b_v, out_w, out_b, ln_g, ln_b, out
+):
+    nc = tc.nc
+    kv_v = kv_in.rearrange("(p s) k -> p s k", s=NSUB)
+    q_v = q_in.rearrange("(p s) c -> p s c", s=NSUB)
+    out_v = out.rearrange("(p s) c -> p s c", s=NSUB)
+    wv_v = w_v.rearrange("(g m t) k -> m g t k", g=4, t=4)
+    ow_v = out_w.rearrange("(n r m) k -> m n r k", n=4, r=4)
+    aw_v = attn_w.rearrange("(p s) h o -> p (s h o)", s=NSUB)
+
+    with ExitStack() as ctx:
+        const = ctx.enter_context(tc.tile_pool(name="const", bufs=1))
+        sb = ctx.enter_context(tc.tile_pool(name="sb", bufs=2))
+        ps = ctx.enter_context(tc.psum_pool(name="ps", bufs=2))
+        if MANUAL:
+            ctx.enter_context(tc.manual_schedule())
+
+        aw_all = const.tile([P, NSUB, 32], BF16, name="aw_all")
+        nc.sync.dma_start(out=aw_all[:].rearrange("p s h -> p (s h)"), in_=aw_v)
+        ident_f = const.tile([P, P], F32, name="ident_f")
+        make_identity(nc, ident_f[:])
+        ident_b = const.tile([P, P], BF16, name="ident_b")
+        make_identity(nc, ident_b[:])
+        bv_raw = const.tile([P, 4, 4], BF16, name="bv_raw")
+        bv = const.tile([P, 16], F32, name="bv")
+        mhalf = const.tile([P, 1], F32, name="mhalf")
+        nc.vector.memset(mhalf[:], -0.5)
+        g_bc = const.tile([P, D], BF16, name="g_bc")
+        b_bc = const.tile([P, D], BF16, name="b_bc")
+        ob_bc = const.tile([P, D], BF16, name="ob_bc")
+        junk = const.tile([P, D], BF16, name="junk")
+        junk4 = const.tile([P, 4], F32, name="junk4")
+        z0 = const.tile([P, D], F32, name="z0")
+        z1 = const.tile([P, D], F32, name="z1")
+        z2 = const.tile([P, D], F32, name="z2")
+        zring = [z0, z1, z2]
+
+        wv_c = const.tile([P, 4, 4, 512], U32, name="wv_c", align_bytes=64)
+        wv_p = const.tile([P, 4, 512], U8, name="wv_p", align_bytes=64)
+        ow_c = const.tile([P, 4, 4, 512], U32, name="ow_c", align_bytes=64)
+        ow_p = const.tile([P, 4, 512], U8, name="ow_p", align_bytes=64)
+
+        def rows(plane, g, lo, hi):
+            if g == 0:
+                return plane[:, lo:hi]
+            return plane[4 * g : P, lo:hi]
+
+        def run_load(r):
+            if r["kind"] == "kv":
+                raw = sb.tile([P, D], BF16, name="raw", tag="raw", bufs=3)
+            elif r["idx"] % 2 == 0:
+                raw = sb.tile([P, D], BF16, name="wraw", tag="oh", bufs=4)
+            else:
+                raw = sb.tile([P, D], BF16, name="wraw", tag="qt", bufs=3)
+            nc.sync.dma_start(out=raw[:], in_=r["src"])
+            r["raw"] = raw
+
+        def run_sort(r):
+            words = r["raw"][:].bitcast(F32)
+            srt = sb.tile([P, 1024], F32, name="srt", tag="srt", bufs=2)
+            nc.scalar.copy(
+                out=srt[:].rearrange("p (u j) -> p u j", u=2),
+                in_=words.rearrange("p (j u) -> p u j", u=2),
+            )
+            r["srt"] = srt
+
+        def run_transposes(r, h, tag, bufs):
+            tp = ps.tile([P, 512], F32, name="tp", tag=tag, bufs=bufs)
+            for gl in range(2):
+                g = 2 * h + gl
+                for u in range(2):
+                    if r["sorted"]:
+                        src = r["srt"][:, 512 * u + 128 * g : 512 * u + 128 * g + 128]
+                    else:
+                        src = r["raw"][:].bitcast(F32)[:, 256 * g + u : 256 * (g + 1) : 2]
+                    c0 = 128 * (2 * gl + u)
+                    nc.tensor.transpose(tp[:, c0 : c0 + 128], src, ident_f[:])
+            r["tp%d" % h] = tp
+
+        def run_evac(r, h, eng):
+            if h == 0:
+                grp = sb.tile([P, D], BF16, name="grp", tag="grp", bufs=3, align_bytes=64)
+                r["grp"] = grp
+            gw = r["grp"][:].bitcast(F32)
+            dst = gw[:, 512 * h : 512 * h + 512].rearrange("p (g r u) -> p g r u", g=2, u=2)
+            src = r["tp%d" % h][:].rearrange("p (g u r) -> p g r u", g=2, u=2)
+            if eng == "s":
+                nc.scalar.copy(out=dst, in_=src)
+            else:
+                nc.vector.tensor_copy(out=dst, in_=src)
+
+        def run_quant(r):
+            c0 = r["col"]
+            for g in range(4):
+                nc.vector.quantize_mx(
+                    out=r["codes"][:, g, c0 : c0 + 128].bitcast(FP8X4),
+                    scales=rows(r["plane"], g, c0, c0 + 128),
+                    in_=r["grp"][:, 512 * g : 512 * g + 512],
+                )
+
+        runs_at = {}
+        loads_at = {}
+
+        def place(r, k_run, k_load):
+            runs_at[k_run] = runs_at.get(k_run, []) + [r]
+            loads_at[k_load] = loads_at.get(k_load, []) + [r]
+
+        wlist = []
+        for g2 in range(4):
+            for t in range(4):
+                wlist.append({"kind": "w", "src": wv_v[:, g2, t, :], "codes": wv_c[:, g2], "plane": wv_p[:, g2],
+                              "col": 128 * t, "sorted": False})
+        for n in range(4):
+            for r4 in range(4):
+                wlist.append({"kind": "w", "src": ow_v[:, n, r4, :], "codes": ow_c[:, n], "plane": ow_p[:, n],
+                              "col": 128 * r4, "sorted": False})
+        for i in range(32):
+            wlist[i]["idx"] = i
+        for i in range(4):
+            place(wlist[i], -14 + 4 * i, -24 + 4 * i)
+        for w in range(28):
+            place(wlist[4 + w], w // 2, w // 2 - 2)
+
+        kvc = {}
+        kvp = {}
+        awt = {}
+        kv_runs = {}
+        for st in range(NSUB):
+            r = {"kind": "kv", "src": kv_v[:, st, :], "col": 128 * (st % 4), "sorted": SORT, "st": st}
+            kv_runs[st] = r
+            place(r, 4 * st - 16, 4 * st - 29)
+
+        ps1 = {}
+        ps2 = {}
+        araw = {}
+        grp2 = {}
+        c2c = {}
+        c2p = {}
+        qt = {}
+        oh = {}
+        s4 = {}
+        nm = {}
+        ssq = {}
+        rstd = {}
+
+        K_FIRST = -29
+        K_LAST = 4 * (NSUB - 1) + LAG2 + 14
+
+        for k in range(K_FIRST, K_LAST + 1):
+            ph = k % 4
+
+            kq = k - (LAG2 + 12)
+            if kq >= 0 and kq % 2 == 0 and kq // 2 < 2 * NSUB:
+                hh = kq // 2
+                nc.sync.dma_start(out=out_v[:, hh // 2, 1024 * (hh % 2) : 1024 * (hh % 2) + 1024], in_=oh[hh][:])
+            for r in loads_at.get(k, []):
+                run_load(r)
+            if k == -20:
+                nc.sync.dma_start(out=bv_raw[:], in_=b_v.rearrange("(g p t) -> p g t", g=4, t=4))
+                nc.vector.tensor_copy(out=bv[:], in_=bv_raw[:].rearrange("p g t -> p (g t)"))
+            if k == 4:
+                nc.sync.dma_start(out=ob_bc[:], in_=out_b.partition_broadcast(P))
+            if k == 6:
+                nc.sync.dma_start(out=g_bc[:], in_=ln_g.partition_broadcast(P))
+            if k == 8:
+                nc.sync.dma_start(out=b_bc[:], in_=ln_b.partition_broadcast(P))
+            kq = k - (LAG2 - 10)
+            if kq >= 0 and kq % 4 == 0 and kq // 4 < NSUB:
+                qq = sb.tile([P, D], BF16, name="qt", tag="qt", bufs=3)
+                nc.sync.dma_start(out=qq[:], in_=q_v[:, kq // 4, :])
+                qt[kq // 4] = qq
+
+            a = k - 1
+            if 0 <= a < 256:
+                b, j = a // 16, a % 16
+                g2, t = j // 4, j % 4
+                if t == 0:
+                    ar = sb.tile([P, 4, 512], BF16, name="araw", tag="araw", bufs=2)
+                    araw[a // 4] = ar
+                nc.vector.scalar_tensor_tensor(
+                    out=araw[a // 4][:, t, :], in0=ps1[a][:], scalar=bv[:, 4 * g2 + t : 4 * g2 + t + 1],
+                    in1=awt[b][:, g2, :], op0=ALU.add, op1=ALU.mult,
+                )
+            c = k - LAG2 - 1
+            if 0 <= c < 256:
+                q, n = c // 4, c % 4
+                if n == 0:
+                    s4t = sb.tile([P, 4], F32, name="s4", tag="s4", bufs=3)
+                    s4[q] = s4t
+                zs = zring[q % 3][:, 512 * n : 512 * n + 512]
+                nc.vector.scalar_tensor_tensor(
+                    out=zs, in0=ps2[c][:], scalar=0.0, in1=zs, op0=ALU.add, op1=ALU.add,
+                    accum_out=s4[q][:, n : n + 1],
+                )
+
+            for r in runs_at.get(k, []):
+                if r["kind"] == "kv":
+                    run_transposes(r, 0, "tp", 2)
+                    run_transposes(r, 1, "tp", 2)
+                    awp = ps.tile([P, 4, P], BF16, name="awp", tag="awp", bufs=1)
+                    for g2 in range(4):
+                        nc.tensor.transpose(awp[:, g2, :], r["awx"][:, 128 * g2 : 128 * g2 + 128], ident_b[:])
+                    r["awp"] = awp
+                else:
+                    run_transposes(r, 0, "ps2", 3)
+                    run_transposes(r, 1, "ps2", 3)
+            a = k
+            if 0 <= a < 256:
+                b, j = a // 16, a % 16
+                g2, t = j // 4, j % 4
+                acc = ps.tile([P, 512], F32, name="ps1", tag="ps1", bufs=2)
+                ps1[a] = acc
+                for g in range(4):
+                    nc.tensor.matmul_mx(
+                        out=acc[:],
+                        lhsT=wv_c[:, g2, g, 128 * t : 128 * t + 128].bitcast(FP8X4),
+                        lhsT_scale=rows(wv_p[:, g2], g, 128 * t, 128 * t + 128),
+                        rhs=kvc[b][:, g, :].bitcast(FP8X4),
+                        rhs_scale=rows(kvp[b], g, 0, 512),
+                        start=(g == 0), stop=(g == 3),
+                    )
+            c = k - LAG2
+            if 0 <= c < 256:
+                b, s, n = c // 16, (c % 16) // 4, c % 4
+                acc = ps.tile([P, 512], F32, name="ps2", tag="ps2", bufs=3)
+                ps2[c] = acc
+                for g in range(4):
+                    nc.tensor.matmul_mx(
+                        out=acc[:],
+                        lhsT=c2c[b][:, g, 128 * s : 128 * s + 128].bitcast(FP8X4),
+                        lhsT_scale=rows(c2p[b], g, 128 * s, 128 * s + 128),
+                        rhs=ow_c[:, n, g, :].bitcast(FP8X4),
+                        rhs_scale=rows(ow_p[:, n], g, 0, 512),
+                        start=(g == 0), stop=(g == 3),
+                    )
+
+            for r in runs_at.get(k, []):
+                if r["kind"] == "kv":
+                    st = r["st"]
+                    run_evac(r, 0, "s")
+                    run_evac(r, 1, "s")
+                    if st % 4 == 0:
+                        at = sb.tile([P, 4, 512], BF16, name="awt", tag="awt", bufs=2)
+                        awt[st // 4] = at
+                    s0 = 128 * (st % 4)
+                    nc.scalar.copy(out=awt[st // 4][:, :, s0 : s0 + 128], in_=r["awp"][:])
+                else:
+                    run_evac(r, 0, "s")
+                    run_evac(r, 1, "s")
+            if ph == 1:
+                gi = (k - 5) // 4
+                if 0 <= gi < 64:
+                    g2t = sb.tile([P, D], BF16, name="grp2", tag="grp2", bufs=1, align_bytes=64)
+                    grp2[gi] = g2t
+                    nc.scalar.copy(
+                        out=g2t[:].rearrange("p (r t) -> p r t", t=4),
+                        in_=araw[gi][:].rearrange("p t r -> p r t"),
+                    )
+                q = (k - LAG2 - 5) // 4
+                if 0 <= q < NSUB:
+                    nmt = sb.tile([P, 1], F32, name="nm", tag="nm", bufs=4)
+                    nm[q] = nmt
+                    nc.scalar.activation(out=junk4[:], in_=s4[q][:], func=ACT.Copy, scale=-1.0 / D, accum_out=nmt[:])
+            if ph == 2:
+                q = (k - LAG2 - 6) // 4
+                if 0 <= q < NSUB:
+                    sq = sb.tile([P, 1], F32, name="ssq", tag="ssq", bufs=3)
+                    ssq[q] = sq
+                    nc.scalar.activation(out=junk[:], in_=zring[q % 3][:], func=ACT.Square, bias=nm[q][:], scale=1.0,
+                                         accum_out=sq[:])
+            if ph == 3:
+                st = (k + 1) // 4 + 5
+                if 0 <= st < NSUB:
+                    r = kv_runs[st]
+                    if SORT:
+                        run_sort(r)
+                    awx = sb.tile([P, 512], BF16, name="awx", tag="awx", bufs=2)
+                    nc.scalar.copy(
+                        out=awx[:].rearrange("p (h r) -> p h r", r=16),
+                        in_=aw_all[:, st, :].unsqueeze(2).to_broadcast([P, 32, 16]),
+                    )
+                    r["awx"] = awx
+
+            for r in runs_at.get(k - 1, []):
+                if r["kind"] == "kv":
+                    st = r["st"]
+                    if st % 4 == 0:
+                        cc = sb.tile([P, 4, 512], U32, name="kvc", tag="kvc", bufs=2, align_bytes=64)
+                        pp = sb.tile([P, 512], U8, name="kvp", tag="kvp", bufs=2, align_bytes=64)
+                        kvc[st // 4] = cc
+                        kvp[st // 4] = pp
+                    r["codes"] = kvc[st // 4]
+                    r["plane"] = kvp[st // 4]
+                run_quant(r)
+            if ph == 3:
+                gi = (k - 7) // 4
+                if 0 <= gi < 64:
+                    b, g2 = gi // 4, gi % 4
+                    if g2 == 0:
+                        cc = sb.tile([P, 4, 512], U32, name="c2c", tag="c2c", bufs=2, align_bytes=64)
+                        pp = sb.tile([P, 512], U8, name="c2p", tag="c2p", bufs=2, align_bytes=64)
+                        c2c[b] = cc
+                        c2p[b] = pp
+                    nc.vector.quantize_mx(
+                        out=c2c[b][:, g2, :].bitcast(FP8X4),
+                        scales=rows(c2p[b], g2, 0, 512),
+                        in_=grp2[gi][:],
+                    )
+            x = k - LAG2 - 8
+            if 0 <= x < 256:
+                q, n = x // 4, x % 4
+                zs = zring[q % 3][:, 512 * n : 512 * n + 512]
+                nc.vector.scalar_tensor_tensor(
+                    out=zs, in0=zs, scalar=nm[q][:], in1=g_bc[:, 512 * n : 512 * n + 512],
+                    op0=ALU.add, op1=ALU.mult,
+                )
+            x = k - LAG2 - 10
+            if 0 <= x < 256:
+                q, n = x // 4, x % 4
+                zs = zring[q % 3][:, 512 * n : 512 * n + 512]
+                if n % 2 == 0:
+                    oht = sb.tile([P, 1024], F32, name="oh", tag="oh", bufs=4)
+                    oh[x // 2] = oht
+                nc.vector.scalar_tensor_tensor(
+                    out=oh[x // 2][:, 512 * (n % 2) : 512 * (n % 2) + 512], in0=zs, scalar=rstd[q][:], in1=b_bc[:, 512 * n : 512 * n + 512],
+                    op0=ALU.mult, op1=ALU.add,
+                )
+
+            x = k - (LAG2 - 2)
+            if 0 <= x < 256:
+                q, n = x // 4, x % 4
+                eng = nc.gpsimd if T7_ON_G else nc.vector
+                eng.tensor_tensor(
+                    out=zring[q % 3][:, 512 * n : 512 * n + 512], in0=qt[q][:, 512 * n : 512 * n + 512],
+                    in1=ob_bc[:, 512 * n : 512 * n + 512], op=ALU.add,
+                )
+            x = k - LAG2 - 8
+            if x >= 0 and x % 4 == 0 and x // 4 < NSUB:
+                q = x // 4
+                ve = sb.tile([P, 1], F32, name="ve", tag="ve", bufs=3)
+                nc.gpsimd.tensor_scalar(out=ve[:], in0=ssq[q][:], scalar1=1.0 / D, scalar2=LN_EPS,
+                                        op0=ALU.mult, op1=ALU.add)
+                rs = sb.tile([P, 1], F32, name="rstd", tag="rstd", bufs=4)
+                rstd[q] = rs
+                nc.gpsimd.tensor_tensor(out=rs[:], in0=ve[:], in1=mhalf[:], op=ALU.pow)

@@ -67,6 +67,10 @@ def tile_crossmodalattention_pa_l_kernel(
         ow_c = const.tile([P, 4, 4, 512], U32, name="ow_c", align_bytes=64)
         ow_p = const.tile([P, 4, 512], U8, name="ow_p", align_bytes=64)
 
+        gp0 = ps.tile([P, 1024], BF16, name="gp0", tag="gp0", bufs=1)
+        gp1 = ps.tile([P, 1024], BF16, name="gp1", tag="gp1", bufs=1)
+        gps = [gp0, gp1]
+
         def rows(plane, g, lo, hi):
             if g == 0:
                 return plane[:, lo:hi]
@@ -169,6 +173,7 @@ def tile_crossmodalattention_pa_l_kernel(
         nm = {}
         ssq = {}
         rstd = {}
+        ve = {}
 
         K_FIRST = -29
         K_LAST = 4 * (NSUB - 1) + LAG2 + 14
@@ -220,22 +225,35 @@ def tile_crossmodalattention_pa_l_kernel(
                     accum_out=s4[q][:, n : n + 1],
                 )
 
+            x = k - LAG2 - 8
+            if 0 <= x < 256:
+                q, n = x // 4, x % 4
+                zs = zring[q % 3][:, 512 * n : 512 * n + 512]
+                nc.vector.scalar_tensor_tensor(
+                    out=zs, in0=zs, scalar=nm[q][:], in1=gps[n // 2][:, 512 * (n % 2) : 512 * (n % 2) + 512],
+                    op0=ALU.add, op1=ALU.mult,
+                )
+
+            if k == 9:
+                for n in range(4):
+                    nc.tensor.matmul(out=gps[n // 2][:, 512 * (n % 2) : 512 * (n % 2) + 512], lhsT=ident_b[:],
+                                     rhs=g_bc[:, 512 * n : 512 * n + 512], start=True, stop=True)
             for r in runs_at.get(k, []):
                 if r["kind"] == "kv":
                     run_transposes(r, 0, "tp", 2)
                     run_transposes(r, 1, "tp", 2)
-                    awp = ps.tile([P, 4, P], BF16, name="awp", tag="awp", bufs=1)
+                    awp = ps.tile([P, 4, P], BF16, name="awp", tag="acc", bufs=4)
                     for g2 in range(4):
                         nc.tensor.transpose(awp[:, g2, :], r["awx"][:, 128 * g2 : 128 * g2 + 128], ident_b[:])
                     r["awp"] = awp
                 else:
-                    run_transposes(r, 0, "ps2", 3)
-                    run_transposes(r, 1, "ps2", 3)
+                    run_transposes(r, 0, "acc", 4)
+                    run_transposes(r, 1, "acc", 4)
             a = k
             if 0 <= a < 256:
                 b, j = a // 16, a % 16
                 g2, t = j // 4, j % 4
-                acc = ps.tile([P, 512], F32, name="ps1", tag="ps1", bufs=2)
+                acc = ps.tile([P, 512], F32, name="ps1", tag="acc", bufs=4)
                 ps1[a] = acc
                 for g in range(4):
                     nc.tensor.matmul_mx(
@@ -249,7 +267,7 @@ def tile_crossmodalattention_pa_l_kernel(
             c = k - LAG2
             if 0 <= c < 256:
                 b, s, n = c // 16, (c % 16) // 4, c % 4
-                acc = ps.tile([P, 512], F32, name="ps2", tag="ps2", bufs=3)
+                acc = ps.tile([P, 512], F32, name="ps2", tag="acc", bufs=4)
                 ps2[c] = acc
                 for g in range(4):
                     nc.tensor.matmul_mx(
@@ -295,6 +313,9 @@ def tile_crossmodalattention_pa_l_kernel(
                     ssq[q] = sq
                     nc.scalar.activation(out=junk[:], in_=zring[q % 3][:], func=ACT.Square, bias=nm[q][:], scale=1.0,
                                          accum_out=sq[:])
+                    vet = sb.tile([P, 1], F32, name="ve", tag="ve", bufs=3)
+                    ve[q] = vet
+                    nc.scalar.activation(out=vet[:], in_=sq[:], func=ACT.Copy, bias=LN_EPS, scale=1.0 / D)
             if ph == 3:
                 st = (k + 1) // 4 + 5
                 if 0 <= st < NSUB:
@@ -333,14 +354,6 @@ def tile_crossmodalattention_pa_l_kernel(
                         scales=rows(c2p[b], g2, 0, 512),
                         in_=grp2[gi][:],
                     )
-            x = k - LAG2 - 8
-            if 0 <= x < 256:
-                q, n = x // 4, x % 4
-                zs = zring[q % 3][:, 512 * n : 512 * n + 512]
-                nc.vector.scalar_tensor_tensor(
-                    out=zs, in0=zs, scalar=nm[q][:], in1=g_bc[:, 512 * n : 512 * n + 512],
-                    op0=ALU.add, op1=ALU.mult,
-                )
             x = k - LAG2 - 10
             if 0 <= x < 256:
                 q, n = x // 4, x % 4
@@ -364,9 +377,6 @@ def tile_crossmodalattention_pa_l_kernel(
             x = k - LAG2 - 8
             if x >= 0 and x % 4 == 0 and x // 4 < NSUB:
                 q = x // 4
-                ve = sb.tile([P, 1], F32, name="ve", tag="ve", bufs=3)
-                nc.gpsimd.tensor_scalar(out=ve[:], in0=ssq[q][:], scalar1=1.0 / D, scalar2=LN_EPS,
-                                        op0=ALU.mult, op1=ALU.add)
                 rs = sb.tile([P, 1], F32, name="rstd", tag="rstd", bufs=4)
                 rstd[q] = rs
-                nc.gpsimd.tensor_tensor(out=rs[:], in0=ve[:], in1=mhalf[:], op=ALU.pow)
+                nc.gpsimd.tensor_tensor(out=rs[:], in0=ve[q][:], in1=mhalf[:], op=ALU.pow)

@@ -52,14 +52,13 @@ def tile_crossmodalattention_pa_l_kernel(
         bv = const.tile([P, 16], F32, name="bv")
         mhalf = const.tile([P, 1], F32, name="mhalf")
         nc.vector.memset(mhalf[:], -0.5)
-        g_bc = const.tile([P, D], BF16, name="g_bc")
         b_bc = const.tile([P, D], BF16, name="b_bc")
         ob_bc = const.tile([P, D], BF16, name="ob_bc")
         junk = const.tile([P, D], BF16, name="junk")
         junk4 = const.tile([P, 4], F32, name="junk4")
-        z0 = const.tile([P, D], F32, name="z0")
-        z1 = const.tile([P, D], F32, name="z1")
-        z2 = const.tile([P, D], F32, name="z2")
+        z0 = const.tile([P, D], F32, name="z0", align_bytes=64)
+        z1 = const.tile([P, D], F32, name="z1", align_bytes=64)
+        z2 = const.tile([P, D], F32, name="z2", align_bytes=64)
         zring = [z0, z1, z2]
 
         wv_c = const.tile([P, 4, 4, 512], U32, name="wv_c", align_bytes=64)
@@ -109,11 +108,16 @@ def tile_crossmodalattention_pa_l_kernel(
             r["tp%d" % h] = tp
 
         def run_evac(r, h, eng):
-            if h == 0:
-                grp = sb.tile([P, D], BF16, name="grp", tag="grp", bufs=3, align_bytes=64)
-                r["grp"] = grp
-            gw = r["grp"][:].bitcast(F32)
-            dst = gw[:, 512 * h : 512 * h + 512].rearrange("p (g r u) -> p g r u", g=2, u=2)
+            e = r["par"]
+            if h == 0 and e == 0:
+                if r["kind"] == "kv":
+                    grp = sb.tile([P, 4, 1024], BF16, name="grp", tag="grp", bufs=2, align_bytes=64)
+                    r["grp"] = grp[:]
+                else:
+                    r["grp"] = zring[(r["idx"] // 2) % 3][:].bitcast(BF16).rearrange("p (g c) -> p g c", g=4)
+                r["mate"]["grp"] = r["grp"]
+            dst = r["grp"][:, 2 * h : 2 * h + 2, 512 * e : 512 * e + 512].bitcast(F32).rearrange(
+                "p g (r u) -> p g r u", u=2)
             src = r["tp%d" % h][:].rearrange("p (g u r) -> p g r u", g=2, u=2)
             if eng == "s":
                 nc.scalar.copy(out=dst, in_=src)
@@ -121,12 +125,12 @@ def tile_crossmodalattention_pa_l_kernel(
                 nc.vector.tensor_copy(out=dst, in_=src)
 
         def run_quant(r):
-            c0 = r["col"]
+            c0 = r["col"] - 128
             for g in range(4):
                 nc.vector.quantize_mx(
-                    out=r["codes"][:, g, c0 : c0 + 128].bitcast(FP8X4),
-                    scales=rows(r["plane"], g, c0, c0 + 128),
-                    in_=r["grp"][:, 512 * g : 512 * g + 512],
+                    out=r["codes"][:, g, c0 : c0 + 256].bitcast(FP8X4),
+                    scales=rows(r["plane"], g, c0, c0 + 256),
+                    in_=r["grp"][:, g, :],
                 )
 
         runs_at = {}
@@ -147,6 +151,8 @@ def tile_crossmodalattention_pa_l_kernel(
                               "col": 128 * r4, "sorted": False})
         for i in range(32):
             wlist[i]["idx"] = i
+            wlist[i]["par"] = i % 2
+            wlist[i]["mate"] = wlist[i + 1 - 2 * (i % 2)]
         for i in range(4):
             place(wlist[i], -14 + 4 * i, -24 + 4 * i)
         for w in range(28):
@@ -158,8 +164,11 @@ def tile_crossmodalattention_pa_l_kernel(
         kv_runs = {}
         for st in range(NSUB):
             r = {"kind": "kv", "src": kv_v[:, st, :], "col": 128 * (st % 4), "sorted": SORT, "st": st}
+            r["par"] = st % 2
             kv_runs[st] = r
             place(r, 4 * st - 16, 4 * st - 29)
+        for st in range(NSUB):
+            kv_runs[st]["mate"] = kv_runs[st + 1 - 2 * (st % 2)]
 
         ps1 = {}
         ps2 = {}
@@ -176,12 +185,12 @@ def tile_crossmodalattention_pa_l_kernel(
         ve = {}
 
         K_FIRST = -29
-        K_LAST = 4 * (NSUB - 1) + LAG2 + 14
+        K_LAST = 4 * (NSUB - 1) + LAG2 + 12
 
         for k in range(K_FIRST, K_LAST + 1):
             ph = k % 4
 
-            kq = k - (LAG2 + 12)
+            kq = k - (LAG2 + 10)
             if kq >= 0 and kq % 2 == 0 and kq // 2 < 2 * NSUB:
                 hh = kq // 2
                 nc.sync.dma_start(out=out_v[:, hh // 2, 1024 * (hh % 2) : 1024 * (hh % 2) + 1024], in_=oh[hh][:])
@@ -193,10 +202,10 @@ def tile_crossmodalattention_pa_l_kernel(
             if k == 4:
                 nc.sync.dma_start(out=ob_bc[:], in_=out_b.partition_broadcast(P))
             if k == 6:
-                nc.sync.dma_start(out=g_bc[:], in_=ln_g.partition_broadcast(P))
+                nc.sync.dma_start(out=junk[:], in_=ln_g.partition_broadcast(P))
             if k == 8:
                 nc.sync.dma_start(out=b_bc[:], in_=ln_b.partition_broadcast(P))
-            kq = k - (LAG2 - 10)
+            kq = k - (LAG2 - 11)
             if kq >= 0 and kq % 4 == 0 and kq // 4 < NSUB:
                 qq = sb.tile([P, D], BF16, name="qt", tag="qt", bufs=3)
                 nc.sync.dma_start(out=qq[:], in_=q_v[:, kq // 4, :])
@@ -226,18 +235,17 @@ def tile_crossmodalattention_pa_l_kernel(
                 )
 
             x = k - LAG2 - 8
-            if 0 <= x < 256:
-                q, n = x // 4, x % 4
-                zs = zring[q % 3][:, 512 * n : 512 * n + 512]
+            if 0 <= x < 256 and x % 2 == 0:
+                q, h = x // 4, (x % 4) // 2
+                zs = zring[q % 3][:, 1024 * h : 1024 * h + 1024]
                 nc.vector.scalar_tensor_tensor(
-                    out=zs, in0=zs, scalar=nm[q][:], in1=gps[n // 2][:, 512 * (n % 2) : 512 * (n % 2) + 512],
-                    op0=ALU.add, op1=ALU.mult,
+                    out=zs, in0=zs, scalar=nm[q][:], in1=gps[h][:], op0=ALU.add, op1=ALU.mult,
                 )
 
             if k == 9:
                 for n in range(4):
                     nc.tensor.matmul(out=gps[n // 2][:, 512 * (n % 2) : 512 * (n % 2) + 512], lhsT=ident_b[:],
-                                     rhs=g_bc[:, 512 * n : 512 * n + 512], start=True, stop=True)
+                                     rhs=junk[:, 512 * n : 512 * n + 512], start=True, stop=True)
             for r in runs_at.get(k, []):
                 if r["kind"] == "kv":
                     run_transposes(r, 0, "tp", 2)
@@ -330,16 +338,17 @@ def tile_crossmodalattention_pa_l_kernel(
                     r["awx"] = awx
 
             for r in runs_at.get(k - 1, []):
-                if r["kind"] == "kv":
+                if r["par"] == 1 and r["kind"] == "kv":
                     st = r["st"]
-                    if st % 4 == 0:
+                    if st % 4 == 1:
                         cc = sb.tile([P, 4, 512], U32, name="kvc", tag="kvc", bufs=2, align_bytes=64)
                         pp = sb.tile([P, 512], U8, name="kvp", tag="kvp", bufs=2, align_bytes=64)
                         kvc[st // 4] = cc
                         kvp[st // 4] = pp
                     r["codes"] = kvc[st // 4]
                     r["plane"] = kvp[st // 4]
-                run_quant(r)
+                if r["par"] == 1:
+                    run_quant(r)
             if ph == 3:
                 gi = (k - 7) // 4
                 if 0 <= gi < 64:
@@ -354,27 +363,26 @@ def tile_crossmodalattention_pa_l_kernel(
                         scales=rows(c2p[b], g2, 0, 512),
                         in_=grp2[gi][:],
                     )
-            x = k - LAG2 - 10
-            if 0 <= x < 256:
-                q, n = x // 4, x % 4
-                zs = zring[q % 3][:, 512 * n : 512 * n + 512]
-                if n % 2 == 0:
-                    oht = sb.tile([P, 1024], F32, name="oh", tag="oh", bufs=4)
-                    oh[x // 2] = oht
+            x = k - LAG2 - 9
+            if 0 <= x < 256 and x % 2 == 0:
+                q, h = x // 4, (x % 4) // 2
+                zs = zring[q % 3][:, 1024 * h : 1024 * h + 1024]
+                oht = sb.tile([P, 1024], F32, name="oh", tag="oh", bufs=4)
+                oh[x // 2] = oht
                 nc.vector.scalar_tensor_tensor(
-                    out=oh[x // 2][:, 512 * (n % 2) : 512 * (n % 2) + 512], in0=zs, scalar=rstd[q][:], in1=b_bc[:, 512 * n : 512 * n + 512],
+                    out=oht[:], in0=zs, scalar=rstd[q][:], in1=b_bc[:, 1024 * h : 1024 * h + 1024],
                     op0=ALU.mult, op1=ALU.add,
                 )
 
-            x = k - (LAG2 - 2)
-            if 0 <= x < 256:
-                q, n = x // 4, x % 4
+            x = k - (LAG2 - 3)
+            if 0 <= x < 256 and x % 2 == 0:
+                q, h = x // 4, (x % 4) // 2
                 eng = nc.gpsimd if T7_ON_G else nc.vector
                 eng.tensor_tensor(
-                    out=zring[q % 3][:, 512 * n : 512 * n + 512], in0=qt[q][:, 512 * n : 512 * n + 512],
-                    in1=ob_bc[:, 512 * n : 512 * n + 512], op=ALU.add,
+                    out=zring[q % 3][:, 1024 * h : 1024 * h + 1024], in0=qt[q][:, 1024 * h : 1024 * h + 1024],
+                    in1=ob_bc[:, 1024 * h : 1024 * h + 1024], op=ALU.add,
                 )
-            x = k - LAG2 - 8
+            x = k - LAG2 - 7
             if x >= 0 and x % 4 == 0 and x // 4 < NSUB:
                 q = x // 4
                 rs = sb.tile([P, 1], F32, name="rstd", tag="rstd", bufs=4)

@@ -55,7 +55,6 @@ def tile_crossmodalattention_pa_l_kernel(
         b_bc = const.tile([P, D], BF16, name="b_bc")
         ob_bc = const.tile([P, D], BF16, name="ob_bc")
         junk = const.tile([P, D], BF16, name="junk")
-        junk4 = const.tile([P, 4], F32, name="junk4")
         z0 = const.tile([P, D], F32, name="z0", align_bytes=64)
         z1 = const.tile([P, D], F32, name="z1", align_bytes=64)
         z2 = const.tile([P, D], F32, name="z2", align_bytes=64)
@@ -178,7 +177,6 @@ def tile_crossmodalattention_pa_l_kernel(
         c2p = {}
         qt = {}
         oh = {}
-        s4 = {}
         nm = {}
         ssq = {}
         rstd = {}
@@ -225,14 +223,8 @@ def tile_crossmodalattention_pa_l_kernel(
             c = k - LAG2 - 1
             if 0 <= c < 256:
                 q, n = c // 4, c % 4
-                if n == 0:
-                    s4t = sb.tile([P, 4], F32, name="s4", tag="s4", bufs=3)
-                    s4[q] = s4t
                 zs = zring[q % 3][:, 512 * n : 512 * n + 512]
-                nc.vector.scalar_tensor_tensor(
-                    out=zs, in0=ps2[c][:], scalar=0.0, in1=zs, op0=ALU.add, op1=ALU.add,
-                    accum_out=s4[q][:, n : n + 1],
-                )
+                nc.vector.tensor_tensor(out=zs, in0=ps2[c][:], in1=zs, op=ALU.add)
 
             x = k - LAG2 - 8
             if 0 <= x < 256 and x % 2 == 0:
@@ -250,9 +242,9 @@ def tile_crossmodalattention_pa_l_kernel(
                 if r["kind"] == "kv":
                     run_transposes(r, 0, "tp", 2)
                     run_transposes(r, 1, "tp", 2)
-                    awp = ps.tile([P, 4, P], BF16, name="awp", tag="acc", bufs=4)
-                    for g2 in range(4):
-                        nc.tensor.transpose(awp[:, g2, :], r["awx"][:, 128 * g2 : 128 * g2 + 128], ident_b[:])
+                    awp = ps.tile([P, 2, P], F32, name="awp", tag="acc", bufs=4)
+                    for w in range(2):
+                        nc.tensor.transpose(awp[:, w, :], r["awx"][:].bitcast(F32)[:, 128 * w : 128 * w + 128], ident_f[:])
                     r["awp"] = awp
                 else:
                     run_transposes(r, 0, "acc", 4)
@@ -296,7 +288,10 @@ def tile_crossmodalattention_pa_l_kernel(
                         at = sb.tile([P, 4, 512], BF16, name="awt", tag="awt", bufs=2)
                         awt[st // 4] = at
                     s0 = 128 * (st % 4)
-                    nc.scalar.copy(out=awt[st // 4][:, :, s0 : s0 + 128], in_=r["awp"][:])
+                    nc.scalar.copy(
+                        out=awt[st // 4][:, :, s0 : s0 + 128].rearrange("p (e w) r -> p e w r", e=2),
+                        in_=r["awp"][:].rearrange("p w r -> p (w r)").bitcast(BF16).rearrange("p (w r e) -> p e w r", w=2, e=2),
+                    )
                 else:
                     run_evac(r, 0, "s")
                     run_evac(r, 1, "s")
@@ -313,7 +308,7 @@ def tile_crossmodalattention_pa_l_kernel(
                 if 0 <= q < NSUB:
                     nmt = sb.tile([P, 1], F32, name="nm", tag="nm", bufs=4)
                     nm[q] = nmt
-                    nc.scalar.activation(out=junk4[:], in_=s4[q][:], func=ACT.Copy, scale=-1.0 / D, accum_out=nmt[:])
+                    nc.scalar.activation(out=junk[:], in_=zring[q % 3][:], func=ACT.Copy, scale=-1.0 / D, accum_out=nmt[:])
             if ph == 2:
                 q = (k - LAG2 - 6) // 4
                 if 0 <= q < NSUB:
@@ -330,12 +325,6 @@ def tile_crossmodalattention_pa_l_kernel(
                     r = kv_runs[st]
                     if SORT:
                         run_sort(r)
-                    awx = sb.tile([P, 512], BF16, name="awx", tag="awx", bufs=2)
-                    nc.scalar.copy(
-                        out=awx[:].rearrange("p (h r) -> p h r", r=16),
-                        in_=aw_all[:, st, :].unsqueeze(2).to_broadcast([P, 32, 16]),
-                    )
-                    r["awx"] = awx
 
             for r in runs_at.get(k - 1, []):
                 if r["par"] == 1 and r["kind"] == "kv":
@@ -382,6 +371,16 @@ def tile_crossmodalattention_pa_l_kernel(
                     out=zring[q % 3][:, 1024 * h : 1024 * h + 1024], in0=qt[q][:, 1024 * h : 1024 * h + 1024],
                     in1=ob_bc[:, 1024 * h : 1024 * h + 1024], op=ALU.add,
                 )
+            if ph == 1:
+                st = (k + 23) // 4
+                if 0 <= st < NSUB:
+                    awx = sb.tile([P, 512], BF16, name="awx", tag="awx", bufs=2)
+                    nc.gpsimd.tensor_scalar(
+                        out=awx[:].rearrange("p (a r e) -> p a r e", r=16, e=2),
+                        in0=aw_all[:, st, :].rearrange("p (e a) -> p a e", e=2).unsqueeze(2).to_broadcast([P, 16, 16, 2]),
+                        scalar1=1.0, scalar2=0.0, op0=ALU.mult, op1=ALU.add,
+                    )
+                    kv_runs[st]["awx"] = awx
             x = k - LAG2 - 7
             if x >= 0 and x % 4 == 0 and x // 4 < NSUB:
                 q = x // 4

from contextlib import ExitStack

import concourse.mybir as mybir
from concourse.masks import make_identity

FLOPS = 2 * 2 * 8192 * 2048 * 2048

F32 = mybir.dt.float32
BF16 = mybir.dt.bfloat16
U32 = mybir.dt.uint32
U8 = mybir.dt.uint8
FP8X4 = mybir.dt.float8_e4m3fn_x4
ALU = mybir.AluOpType
ACT = mybir.ActivationFunctionType

P = 128
D = 2048
NSUB = 64
LN_EPS = 1e-5

SORT = True
T7_ON_G = True
MANUAL = True
LAG2 = 20


def tile_crossmodalattention_pa_l_kernel(
    tc, kv_in, q_in, attn_w, w_v, b_v, out_w, out_b, ln_g, ln_b, out
):
    nc = tc.nc
    kv_v = kv_in.rearrange("(p s) k -> p s k", s=NSUB)
    q_v = q_in.rearrange("(p s) c -> p s c", s=NSUB)
    out_v = out.rearrange("(p s) c -> p s c", s=NSUB)
    wv_v = w_v.rearrange("(g m t) k -> m g t k", g=4, t=4)
    ow_v = out_w.rearrange("(n r m) k -> m n r k", n=4, r=4)
    aw_v = attn_w.rearrange("(p s) h o -> p (s h o)", s=NSUB)

    with ExitStack() as ctx:
        const = ctx.enter_context(tc.tile_pool(name="const", bufs=1))
        sb = ctx.enter_context(tc.tile_pool(name="sb", bufs=2))
        ps = ctx.enter_context(tc.psum_pool(name="ps", bufs=2))
        if MANUAL:
            ctx.enter_context(tc.manual_schedule())

        aw_all = const.tile([P, NSUB, 32], BF16, name="aw_all")
        nc.sync.dma_start(out=aw_all[:].rearrange("p s h -> p (s h)"), in_=aw_v)
        ident_f = const.tile([P, P], F32, name="ident_f")
        make_identity(nc, ident_f[:])
        ident_b = const.tile([P, P], BF16, name="ident_b")
        make_identity(nc, ident_b[:])
        bv_raw = const.tile([P, 4, 4], BF16, name="bv_raw")
        bv = const.tile([P, 16], F32, name="bv")
        mhalf = const.tile([P, 1], F32, name="mhalf")
        nc.vector.memset(mhalf[:], -0.5)
        b_bc = const.tile([P, D], BF16, name="b_bc")
        ob_bc = const.tile([P, D], BF16, name="ob_bc")
        junk = const.tile([P, D], BF16, name="junk")
        z0 = const.tile([P, D], F32, name="z0", align_bytes=64)
        z1 = const.tile([P, D], F32, name="z1", align_bytes=64)
        z2 = const.tile([P, D], F32, name="z2", align_bytes=64)
        zring = [z0, z1, z2]

        wv_c = const.tile([P, 4, 4, 512], U32, name="wv_c", align_bytes=64)
        wv_p = const.tile([P, 4, 512], U8, name="wv_p", align_bytes=64)
        ow_c = const.tile([P, 4, 4, 512], U32, name="ow_c", align_bytes=64)
        ow_p = const.tile([P, 4, 512], U8, name="ow_p", align_bytes=64)

        gp0 = ps.tile([P, 1024], BF16, name="gp0", tag="gp0", bufs=1)
        gp1 = ps.tile([P, 1024], BF16, name="gp1", tag="gp1", bufs=1)
        gps = [gp0, gp1]

        def rows(plane, g, lo, hi):
            if g == 0:
                return plane[:, lo:hi]
            return plane[4 * g : P, lo:hi]

        def run_load(r):
            if r["kind"] == "kv":
                raw = sb.tile([P, D], BF16, name="raw", tag="raw", bufs=3)
            elif r["idx"] % 2 == 0:
                raw = sb.tile([P, D], BF16, name="wraw", tag="oh", bufs=4)
            else:
                raw = sb.tile([P, D], BF16, name="wraw", tag="qt", bufs=3)
            nc.sync.dma_start(out=raw[:], in_=r["src"])
            r["raw"] = raw

        def run_sort(r):
            words = r["raw"][:].bitcast(F32)
            srt = sb.tile([P, 1024], F32, name="srt", tag="srt", bufs=2)
            nc.scalar.copy(
                out=srt[:].rearrange("p (u j) -> p u j", u=2),
                in_=words.rearrange("p (j u) -> p u j", u=2),
            )
            r["srt"] = srt

        def run_transposes(r, h, tag, bufs):
            tp = ps.tile([P, 512], F32, name="tp", tag=tag, bufs=bufs)
            for gl in range(2):
                g = 2 * h + gl
                for u in range(2):
                    if r["sorted"]:
                        src = r["srt"][:, 512 * u + 128 * g : 512 * u + 128 * g + 128]
                    else:
                        src = r["raw"][:].bitcast(F32)[:, 256 * g + u : 256 * (g + 1) : 2]
                    c0 = 128 * (2 * gl + u)
                    nc.tensor.transpose(tp[:, c0 : c0 + 128], src, ident_f[:])
            r["tp%d" % h] = tp

        def run_evac(r, h, eng):
            e = r["par"]
            if h == 0 and e == 0:
                if r["kind"] == "kv":
                    grp = sb.tile([P, 4, 1024], BF16, name="grp", tag="grp", bufs=2, align_bytes=64)
                    r["grp"] = grp[:]
                else:
                    r["grp"] = zring[(r["idx"] // 2) % 3][:].bitcast(BF16).rearrange("p (g c) -> p g c", g=4)
                r["mate"]["grp"] = r["grp"]
            dst = r["grp"][:, 2 * h : 2 * h + 2, 512 * e : 512 * e + 512].bitcast(F32).rearrange(
                "p g (r u) -> p g r u", u=2)
            src = r["tp%d" % h][:].rearrange("p (g u r) -> p g r u", g=2, u=2)
            if eng == "s":
                nc.scalar.copy(out=dst, in_=src)
            else:
                nc.vector.tensor_copy(out=dst, in_=src)

        def run_quant(r):
            c0 = r["col"] - 128
            for g in range(4):
                nc.vector.quantize_mx(
                    out=r["codes"][:, g, c0 : c0 + 256].bitcast(FP8X4),
                    scales=rows(r["plane"], g, c0, c0 + 256),
                    in_=r["grp"][:, g, :],
                )

        runs_at = {}
        loads_at = {}

        def place(r, k_run, k_load):
            runs_at[k_run] = runs_at.get(k_run, []) + [r]
            loads_at[k_load] = loads_at.get(k_load, []) + [r]

        wlist = []
        for g2 in range(4):
            for t in range(4):
                wlist.append({"kind": "w", "src": wv_v[:, g2, t, :], "codes": wv_c[:, g2], "plane": wv_p[:, g2],
                              "col": 128 * t, "sorted": False})
        for n in range(4):
            for r4 in range(4):
                wlist.append({"kind": "w", "src": ow_v[:, n, r4, :], "codes": ow_c[:, n], "plane": ow_p[:, n],
                              "col": 128 * r4, "sorted": False})
        for i in range(32):
            wlist[i]["idx"] = i
            wlist[i]["par"] = i % 2
            wlist[i]["mate"] = wlist[i + 1 - 2 * (i % 2)]
        for i in range(4):
            place(wlist[i], -14 + 4 * i, -24 + 4 * i)
        for w in range(28):
            place(wlist[4 + w], w // 2, w // 2 - 2)

        kvc = {}
        kvp = {}
        awt = {}
        kv_runs = {}
        for st in range(NSUB):
            r = {"kind": "kv", "src": kv_v[:, st, :], "col": 128 * (st % 4), "sorted": SORT, "st": st}
            r["par"] = st % 2
            kv_runs[st] = r
            place(r, 4 * st - 16, 4 * st - 29)
        for st in range(NSUB):
            kv_runs[st]["mate"] = kv_runs[st + 1 - 2 * (st % 2)]

        ps1 = {}
        ps2 = {}
        araw = {}
        grp2 = {}
        c2c = {}
        c2p = {}
        qt = {}
        oh = {}
        nm = {}
        ssq = {}
        rstd = {}
        ve = {}

        K_FIRST = -29
        K_LAST = 4 * (NSUB - 1) + LAG2 + 12

        for k in range(K_FIRST, K_LAST + 1):
            ph = k % 4

            kq = k - (LAG2 + 10)
            if kq >= 0 and kq % 2 == 0 and kq // 2 < 2 * NSUB:
                hh = kq // 2
                nc.sync.dma_start(out=out_v[:, hh // 2, 1024 * (hh % 2) : 1024 * (hh % 2) + 1024], in_=oh[hh][:])
            for r in loads_at.get(k, []):
                run_load(r)
            if k == -20:
                nc.sync.dma_start(out=bv_raw[:], in_=b_v.rearrange("(g p t) -> p g t", g=4, t=4))
                nc.vector.tensor_copy(out=bv[:], in_=bv_raw[:].rearrange("p g t -> p (g t)"))
            if k == 4:
                nc.sync.dma_start(out=ob_bc[:], in_=out_b.partition_broadcast(P))
            if k == 6:
                nc.sync.dma_start(out=junk[:], in_=ln_g.partition_broadcast(P))
            if k == 8:
                nc.sync.dma_start(out=b_bc[:], in_=ln_b.partition_broadcast(P))
            kq = k - (LAG2 - 11)
            if kq >= 0 and kq % 4 == 0 and kq // 4 < NSUB:
                qq = sb.tile([P, D], BF16, name="qt", tag="qt", bufs=3)
                nc.sync.dma_start(out=qq[:], in_=q_v[:, kq // 4, :])
                qt[kq // 4] = qq

            a = k - 1
            if 0 <= a < 256:
                b, j = a // 16, a % 16
                g2, t = j // 4, j % 4
                if t == 0:
                    ar = sb.tile([P, 4, 512], BF16, name="araw", tag="araw", bufs=2)
                    araw[a // 4] = ar
                nc.vector.scalar_tensor_tensor(
                    out=araw[a // 4][:, t, :], in0=ps1[a][:], scalar=bv[:, 4 * g2 + t : 4 * g2 + t + 1],
                    in1=awt[b][:, g2, :], op0=ALU.add, op1=ALU.mult,
                )
            c = k - LAG2 - 1
            if 0 <= c < 256:
                q, n = c // 4, c % 4
                zs = zring[q % 3][:, 512 * n : 512 * n + 512]
                nc.vector.tensor_tensor(out=zs, in0=ps2[c][:], in1=zs, op=ALU.add)

            x = k - LAG2 - 8
            if 0 <= x < 256 and x % 2 == 0:
                q, h = x // 4, (x % 4) // 2
                zs = zring[q % 3][:, 1024 * h : 1024 * h + 1024]
                nc.vector.scalar_tensor_tensor(
                    out=zs, in0=zs, scalar=nm[q][:], in1=gps[h][:], op0=ALU.add, op1=ALU.mult,
                )

            if k == 9:
                for n in range(4):
                    nc.tensor.matmul(out=gps[n // 2][:, 512 * (n % 2) : 512 * (n % 2) + 512], lhsT=ident_b[:],
                                     rhs=junk[:, 512 * n : 512 * n + 512], start=True, stop=True)
            for r in runs_at.get(k, []):
                if r["kind"] == "kv":
                    run_transposes(r, 0, "tp", 2)
                    run_transposes(r, 1, "tp", 2)
                    awp = ps.tile([P, 2, P], F32, name="awp", tag="acc", bufs=4)
                    for w in range(2):
                        nc.tensor.transpose(awp[:, w, :], r["awx"][:].bitcast(F32)[:, 128 * w : 128 * w + 128], ident_f[:])
                    r["awp"] = awp
                else:
                    run_transposes(r, 0, "acc", 4)
                    run_transposes(r, 1, "acc", 4)
            a = k
            if 0 <= a < 256:
                b, j = a // 16, a % 16
                g2, t = j // 4, j % 4
                acc = ps.tile([P, 512], F32, name="ps1", tag="acc", bufs=4)
                ps1[a] = acc
                for g in range(4):
                    nc.tensor.matmul_mx(
                        out=acc[:],
                        lhsT=wv_c[:, g2, g, 128 * t : 128 * t + 128].bitcast(FP8X4),
                        lhsT_scale=rows(wv_p[:, g2], g, 128 * t, 128 * t + 128),
                        rhs=kvc[b][:, g, :].bitcast(FP8X4),
                        rhs_scale=rows(kvp[b], g, 0, 512),
                        start=(g == 0), stop=(g == 3),
                    )
            c = k - LAG2
            if 0 <= c < 256:
                b, s, n = c // 16, (c % 16) // 4, c % 4
                acc = ps.tile([P, 512], F32, name="ps2", tag="acc", bufs=4)
                ps2[c] = acc
                for g in range(4):
                    nc.tensor.matmul_mx(
                        out=acc[:],
                        lhsT=c2c[b][:, g, 128 * s : 128 * s + 128].bitcast(FP8X4),
                        lhsT_scale=rows(c2p[b], g, 128 * s, 128 * s + 128),
                        rhs=ow_c[:, n, g, :].bitcast(FP8X4),
                        rhs_scale=rows(ow_p[:, n], g, 0, 512),
                        start=(g == 0), stop=(g == 3),
                    )

            for r in runs_at.get(k, []):
                if r["kind"] == "kv":
                    st = r["st"]
                    run_evac(r, 0, "s")
                    run_evac(r, 1, "s")
                    if st % 4 == 0:
                        at = sb.tile([P, 4, 512], BF16, name="awt", tag="awt", bufs=2)
                        awt[st // 4] = at
                    s0 = 128 * (st % 4)
                    nc.scalar.copy(
                        out=awt[st // 4][:, :, s0 : s0 + 128].rearrange("p (e w) r -> p e w r", e=2),
                        in_=r["awp"][:].rearrange("p w r -> p (w r)").bitcast(BF16).rearrange("p (w r e) -> p e w r", w=2, e=2),
                    )
                else:
                    run_evac(r, 0, "s")
                    run_evac(r, 1, "s")
            if ph == 1:
                gi = (k - 5) // 4
                if 0 <= gi < 64:
                    g2t = sb.tile([P, D], BF16, name="grp2", tag="grp2", bufs=1, align_bytes=64)
                    grp2[gi] = g2t
                    nc.scalar.copy(
                        out=g2t[:].rearrange("p (r t) -> p r t", t=4),
                        in_=araw[gi][:].rearrange("p t r -> p r t"),
                    )
                q = (k - LAG2 - 5) // 4
                if 0 <= q < NSUB:
                    nmt = sb.tile([P, 1], F32, name="nm", tag="nm", bufs=4)
                    nm[q] = nmt
                    nc.scalar.activation(out=junk[:], in_=zring[q % 3][:], func=ACT.Copy, scale=-1.0 / D, accum_out=nmt[:])
            if ph == 2:
                q = (k - LAG2 - 6) // 4
                if 0 <= q < NSUB:
                    sq = sb.tile([P, 1], F32, name="ssq", tag="ssq", bufs=3)
                    ssq[q] = sq
                    nc.scalar.activation(out=junk[:], in_=zring[q % 3][:], func=ACT.Square, bias=nm[q][:], scale=1.0,
                                         accum_out=sq[:])
                    vet = sb.tile([P, 1], F32, name="ve", tag="ve", bufs=3)
                    ve[q] = vet
                    nc.scalar.activation(out=vet[:], in_=sq[:], func=ACT.Copy, bias=LN_EPS, scale=1.0 / D)
            if ph == 3:
                st = (k + 1) // 4 + 5
                if 0 <= st < NSUB:
                    r = kv_runs[st]
                    if SORT:
                        run_sort(r)

            for r in runs_at.get(k - 1, []):
                if r["par"] == 1 and r["kind"] == "kv":
                    st = r["st"]
                    if st % 4 == 1:
                        cc = sb.tile([P, 4, 512], U32, name="kvc", tag="kvc", bufs=2, align_bytes=64)
                        pp = sb.tile([P, 512], U8, name="kvp", tag="kvp", bufs=2, align_bytes=64)
                        kvc[st // 4] = cc
                        kvp[st // 4] = pp
                    r["codes"] = kvc[st // 4]
                    r["plane"] = kvp[st // 4]
                if r["par"] == 1:
                    run_quant(r)
            if ph == 3:
                gi = (k - 7) // 4
                if 0 <= gi < 64:
                    b, g2 = gi // 4, gi % 4
                    if g2 == 0:
                        cc = sb.tile([P, 4, 512], U32, name="c2c", tag="c2c", bufs=2, align_bytes=64)
                        pp = sb.tile([P, 512], U8, name="c2p", tag="c2p", bufs=2, align_bytes=64)
                        c2c[b] = cc
                        c2p[b] = pp
                    nc.vector.quantize_mx(
                        out=c2c[b][:, g2, :].bitcast(FP8X4),
                        scales=rows(c2p[b], g2, 0, 512),
                        in_=grp2[gi][:],
                    )
            x = k - LAG2 - 9
            if 0 <= x < 256 and x % 2 == 0:
                q, h = x // 4, (x % 4) // 2
                zs = zring[q % 3][:, 1024 * h : 1024 * h + 1024]
                oht = sb.tile([P, 1024], F32, name="oh", tag="oh", bufs=4)
                oh[x // 2] = oht
                nc.vector.scalar_tensor_tensor(
                    out=oht[:], in0=zs, scalar=rstd[q][:], in1=b_bc[:, 1024 * h : 1024 * h + 1024],
                    op0=ALU.mult, op1=ALU.add,
                )

            x = k - (LAG2 - 3)
            if 0 <= x < 256 and x % 2 == 0:
                q, h = x // 4, (x % 4) // 2
                eng = nc.gpsimd if T7_ON_G else nc.vector
                eng.tensor_tensor(
                    out=zring[q % 3][:, 1024 * h : 1024 * h + 1024], in0=qt[q][:, 1024 * h : 1024 * h + 1024],
                    in1=ob_bc[:, 1024 * h : 1024 * h + 1024], op=ALU.add,
                )
            if ph == 1:
                st = (k + 23) // 4
                if 0 <= st < NSUB:
                    awx = sb.tile([P, 512], BF16, name="awx", tag="awx", bufs=2)
                    nc.gpsimd.tensor_scalar(
                        out=awx[:].rearrange("p (a r e) -> p a r e", r=16, e=2),
                        in0=aw_all[:, st, :].rearrange("p (e a) -> p a e", e=2).unsqueeze(2).to_broadcast([P, 16, 16, 2]),
                        scalar1=1.0, scalar2=0.0, op0=ALU.mult, op1=ALU.add,
                    )
                    kv_runs[st]["awx"] = awx
            x = k - LAG2 - 7
            if x >= 0 and x % 4 == 0 and x // 4 < NSUB:
                q = x // 4
                rs = sb.tile([P, 1], F32, name="rstd", tag="rstd", bufs=4)
                rstd[q] = rs
                nc.gpsimd.tensor_tensor(out=rs[:], in0=ve[q][:], in1=mhalf[:], op=ALU.pow)
